import numpy as np
import ml_dtypes


def mxq(x, axis, fmt="e4m3"):
    dtype, down = {"e4m3": (ml_dtypes.float8_e4m3fn, 7), "e5m2": (ml_dtypes.float8_e5m2, 14)}[fmt]
    v = np.moveaxis(np.asarray(x, np.float32).astype(ml_dtypes.bfloat16).astype(np.float64), axis, -1)
    blocks = v.reshape(v.shape[:-1] + (-1, 32))
    amax = np.abs(blocks).max(-1, keepdims=True)
    byte = np.maximum(np.where(amax > 0, np.frexp(amax)[1] - 1 + 127, 0) - down, 1)
    scale = np.exp2(byte - 127.0)
    codes = (blocks / scale).astype(np.float32).astype(dtype).astype(np.float64)
    return np.moveaxis((codes * scale).reshape(v.shape), -1, axis)


WIDE = False


def mx_kscale(k):
    if not WIDE:
        return np.ones(k)
    levels = np.array([20, -20, 10, -10, 0])
    a = np.random.permutation(np.resize(levels, k // 512 * 4)).reshape(k // 512, 4)
    idx = np.arange(k)
    return np.exp2(a[idx // 512, idx % 128 // 32])


BF16 = ml_dtypes.bfloat16


def bf(x):
    return np.asarray(x, np.float32).astype(BF16)


def f64(x):
    return np.asarray(x).astype(np.float64)


B, C, H, W, O = 4, 128, 128, 128, 512
K = 4 * C
T = B * (H // 2) * (W // 2)


def haar_dwt2(x):
    nb, nc_, nh, nw = x.shape
    xr = x.reshape(nb, nc_, nh // 2, 2, nw // 2, 2)
    a = xr[:, :, :, 0, :, 0]
    b = xr[:, :, :, 0, :, 1]
    c = xr[:, :, :, 1, :, 0]
    d = xr[:, :, :, 1, :, 1]
    half = 0.5
    LL = (a + b + c + d) * half
    LH = (a + b - c - d) * half
    HL = (a - b + c - d) * half
    HH = (a - b - c + d) * half
    return LL, LH, HL, HH


def haar_combined(x):
    nb, nc_, nh, nw = x.shape
    LL, LH, HL, HH = haar_dwt2(x)
    return np.stack([LL, LH, HL, HH], axis=2).reshape(nb, nc_ * 4, nh // 2, nw // 2)


def setup_inputs():
    s = mx_kscale(T).reshape(B, 1, H // 2, W // 2)
    sx = np.repeat(np.repeat(s, 2, axis=2), 2, axis=3)
    x = np.random.standard_normal((B, C, H, W)) * sx
    w = np.random.standard_normal((O, K, 1, 1)) / np.sqrt(K)
    e = np.random.randint(-12, 1, (B, 1, H // 2, W // 2))
    g = np.random.standard_normal((B, O, H // 2, W // 2)) * np.exp2(e) * 0.25 / s
    return {"x": bf(x), "w_fusion": bf(w), "grad_out": bf(g)}


def reference(x, w_fusion, grad_out):
    combined = haar_combined(f64(x))
    cm = combined.transpose(1, 0, 2, 3).reshape(K, T)
    gm = f64(grad_out).transpose(1, 0, 2, 3).reshape(O, T)
    gw = mxq(gm, 1, "e5m2") @ mxq(cm, 1, "e4m3").T
    return gw.reshape(O, K, 1, 1)

@@ -1,0 +1,129 @@
+from contextlib import ExitStack
+
+import concourse.mybir as mybir
+from concourse.masks import make_identity
+
+F32 = mybir.dt.float32
+BF16 = mybir.dt.bfloat16
+U32 = mybir.dt.uint32
+U8 = mybir.dt.uint8
+E4M3X4 = mybir.dt.float8_e4m3fn_x4
+E5M2X4 = mybir.dt.float8_e5m2_x4
+ADD = mybir.AluOpType.add
+SUB = mybir.AluOpType.subtract
+COPY = mybir.ActivationFunctionType.Copy
+
+P = 128
+IMAGES = 4
+O = 512
+K = 512
+TOKENS = 16384
+PASS = 512
+CHUNK_PASSES = 4
+CHUNKS = TOKENS // (PASS * CHUNK_PASSES)
+O_TILES = O // P
+
+FLOPS = 2 * O * K * TOKENS
+BYTES = 2 * 2 * K * TOKENS + 4 * O * K
+
+
+def tile_haarwaveletlayer_kernel(tc, x, w_fusion, grad_out, out):
+    nc = tc.nc
+    with ExitStack() as ctx:
+        const = ctx.enter_context(tc.tile_pool(name="const", bufs=1))
+        loads = ctx.enter_context(tc.tile_pool(name="loads", bufs=3))
+        work = ctx.enter_context(tc.tile_pool(name="work", bufs=2))
+        quant = ctx.enter_context(tc.tile_pool(name="quant", bufs=3))
+        acc_pool = ctx.enter_context(tc.psum_pool(name="acc", bufs=1))
+        x_banks = ctx.enter_context(tc.psum_pool(name="xbanks", bufs=1))
+        g_banks = ctx.enter_context(tc.psum_pool(name="gbanks", bufs=2))
+
+        ident = const.tile([P, P], F32)
+        make_identity(nc, ident[:])
+
+        acc = [acc_pool.tile([P, K], F32, name="acc%d" % ot) for ot in range(O_TILES)]
+
+        for ch in range(CHUNKS):
+            n = ch // 2
+            half = ch % 2
+            rows = x[n].rearrange("c (i r) w -> c r i w", r=2)
+            xs = loads.tile([P, 2, 4096], BF16)
+            for r in range(2):
+                nc.sync.dma_start(
+                    out=xs[:, r, :].rearrange("c (i w) -> c i w", w=128),
+                    in_=rows[:, r, 32 * half : 32 * half + 32, :],
+                )
+            gs = loads.tile([P, O_TILES, 2048], BF16)
+            for ot in range(O_TILES):
+                nc.sync.dma_start(
+                    out=gs[:, ot, :],
+                    in_=grad_out[n, ot * P : (ot + 1) * P].rearrange("o i j -> o (i j)")[
+                        :, 2048 * half : 2048 * half + 2048
+                    ],
+                )
+            xw = xs[:].bitcast(F32)
+            gw = gs[:].bitcast(F32)
+
+            for q in range(CHUNK_PASSES):
+                g = ch * CHUNK_PASSES + q
+
+                gg = work.tile([P, 4 * O], BF16, align_bytes=64)
+                ggw = gg[:].bitcast(F32)
+                for hb in range(2):
+                    gt = g_banks.tile([P, 2, 2, P], F32)
+                    for u in range(2):
+                        for a in range(2):
+                            s = 256 * q + 128 * u
+                            nc.tensor.transpose(gt[:, u, a, :], gw[:, 2 * hb + a, s : s + 128], ident[:])
+                    nc.scalar.copy(
+                        out=ggw[:, 512 * hb : 512 * hb + 512].rearrange("p (o u) -> p o u", u=2),
+                        in_=gt[:].rearrange("p u a o -> p (a o) u"),
+                    )
+                gc = quant.tile([P, O], U32, align_bytes=64)
+                gsc = quant.tile([P, O], U8, align_bytes=64)
+                nc.vector.quantize_mx(out=gc[:].bitcast(E5M2X4), scales=gsc[:], in_=gg[:])
+
+                top = x_banks.tile([P, 4, P], F32)
+                bot = x_banks.tile([P, 4, P], F32)
+                for r, bank in ((1, bot), (0, top)):
+                    for t in range(4):
+                        s = 512 * q + 256 * (t // 2) + (t % 2)
+                        nc.tensor.transpose(bank[:, t, :], xw[:, r, s : s + 255 : 2], ident[:])
+                bot_sb = work.tile([P, P, 4], F32)
+                nc.scalar.copy(out=bot_sb[:], in_=bot[:].rearrange("p t c -> p c t"))
+
+                top_px = top[:].bitcast(BF16).rearrange("p t (c h) -> p h c t", h=2)
+                bot_px = bot_sb[:].bitcast(BF16).rearrange("p c (t h) -> p h c t", h=2)
+                sd = work.tile([P, 2, 2, P, 4], F32)
+                nc.vector.tensor_tensor(out=sd[:, 0], in0=top_px, in1=bot_px, op=ADD)
+                nc.vector.tensor_tensor(out=sd[:, 1], in0=top_px, in1=bot_px, op=SUB)
+                gx = work.tile([P, 4, P, 4], BF16, align_bytes=64)
+                nc.vector.tensor_tensor(out=gx[:, 0:2], in0=sd[:, :, 0], in1=sd[:, :, 1], op=ADD)
+                nc.vector.tensor_tensor(out=gx[:, 2:4], in0=sd[:, :, 0], in1=sd[:, :, 1], op=SUB)
+                xc = quant.tile([P, K], U32, align_bytes=64)
+                xsc = quant.tile([P, K], U8, align_bytes=64)
+                nc.vector.quantize_mx(
+                    out=xc[:].bitcast(E4M3X4), scales=xsc[:], in_=gx[:].rearrange("p b c t -> p (b c t)")
+                )
+
+                for ot in range(O_TILES):
+                    cols = slice(ot * P, (ot + 1) * P)
+                    nc.tensor.matmul_mx(
+                        out=acc[ot][:],
+                        lhsT=gc[:, cols].bitcast(E5M2X4),
+                        lhsT_scale=gsc[:, cols],
+                        rhs=xc[:].bitcast(E4M3X4),
+                        rhs_scale=xsc[:],
+                        start=(g == 0),
+                        stop=(g == TOKENS // PASS - 1),
+                    )
+
+        out2 = out.rearrange("o k a b -> o (k a b)")
+        for ot in range(O_TILES):
+            res = work.tile([P, P, 4], F32)
+            banded = acc[ot][:].rearrange("p (b c) -> p c b", b=4)
+            if ot % 2 == 0:
+                nc.scalar.activation(out=res[:], in_=banded, func=COPY, scale=0.5)
+            else:
+                nc.vector.tensor_scalar_mul(res[:], banded, 0.5)
+            nc.sync.dma_start(out=out2[ot * P : (ot + 1) * P, :], in_=res[:].rearrange("p c b -> p (c b)"))

@@ -19,8 +19,7 @@ O = 512
 K = 512
 TOKENS = 16384
 PASS = 512
-CHUNK_PASSES = 4
-CHUNKS = TOKENS // (PASS * CHUNK_PASSES)
+PASSES = TOKENS // PASS
 O_TILES = O // P
 
 FLOPS = 2 * O * K * TOKENS
@@ -32,7 +31,7 @@ def tile_haarwaveletlayer_kernel(tc, x, w_fusion, grad_out, out):
     with ExitStack() as ctx:
         const = ctx.enter_context(tc.tile_pool(name="const", bufs=1))
         loads = ctx.enter_context(tc.tile_pool(name="loads", bufs=3))
-        work = ctx.enter_context(tc.tile_pool(name="work", bufs=2))
+        work = ctx.enter_context(tc.tile_pool(name="work", bufs=3))
         quant = ctx.enter_context(tc.tile_pool(name="quant", bufs=3))
         acc_pool = ctx.enter_context(tc.psum_pool(name="acc", bufs=1))
         x_banks = ctx.enter_context(tc.psum_pool(name="xbanks", bufs=1))
@@ -43,29 +42,29 @@ def tile_haarwaveletlayer_kernel(tc, x, w_fusion, grad_out, out):
 
         acc = [acc_pool.tile([P, K], F32, name="acc%d" % ot) for ot in range(O_TILES)]
 
-        for ch in range(CHUNKS):
-            n = ch // 2
-            half = ch % 2
+        chunks = [(0, 0, 1), (0, 1, 1), (0, 2, 2), (0, 4, 4)]
+        chunks += [(n, f, 4) for n in range(1, IMAGES) for f in (0, 4)]
+        for n, first, count in chunks:
             rows = x[n].rearrange("c (i r) w -> c r i w", r=2)
             xs = loads.tile([P, 2, 4096], BF16)
             for r in range(2):
                 nc.sync.dma_start(
-                    out=xs[:, r, :].rearrange("c (i w) -> c i w", w=128),
-                    in_=rows[:, r, 32 * half : 32 * half + 32, :],
+                    out=xs[:, r, : 1024 * count].rearrange("c (i w) -> c i w", w=128),
+                    in_=rows[:, r, 8 * first : 8 * (first + count), :],
                 )
             gs = loads.tile([P, O_TILES, 2048], BF16)
             for ot in range(O_TILES):
                 nc.sync.dma_start(
-                    out=gs[:, ot, :],
+                    out=gs[:, ot, : PASS * count],
                     in_=grad_out[n, ot * P : (ot + 1) * P].rearrange("o i j -> o (i j)")[
-                        :, 2048 * half : 2048 * half + 2048
+                        :, PASS * first : PASS * (first + count)
                     ],
                 )
             xw = xs[:].bitcast(F32)
             gw = gs[:].bitcast(F32)
 
-            for q in range(CHUNK_PASSES):
-                g = ch * CHUNK_PASSES + q
+            for q in range(count):
+                g = 8 * n + first + q
 
                 gg = work.tile([P, 4 * O], BF16, align_bytes=64)
                 ggw = gg[:].bitcast(F32)
@@ -99,7 +98,7 @@ def tile_haarwaveletlayer_kernel(tc, x, w_fusion, grad_out, out):
                 nc.vector.tensor_tensor(out=sd[:, 1], in0=top_px, in1=bot_px, op=SUB)
                 gx = work.tile([P, 4, P, 4], BF16, align_bytes=64)
                 nc.vector.tensor_tensor(out=gx[:, 0:2], in0=sd[:, :, 0], in1=sd[:, :, 1], op=ADD)
-                nc.vector.tensor_tensor(out=gx[:, 2:4], in0=sd[:, :, 0], in1=sd[:, :, 1], op=SUB)
+                nc.gpsimd.tensor_tensor(out=gx[:, 2:4], in0=sd[:, :, 0], in1=sd[:, :, 1], op=SUB)
                 xc = quant.tile([P, K], U32, align_bytes=64)
                 xsc = quant.tile([P, K], U8, align_bytes=64)
                 nc.vector.quantize_mx(
@@ -115,7 +114,7 @@ def tile_haarwaveletlayer_kernel(tc, x, w_fusion, grad_out, out):
                         rhs=xc[:].bitcast(E4M3X4),
                         rhs_scale=xsc[:],
                         start=(g == 0),
-                        stop=(g == TOKENS // PASS - 1),
+                        stop=(g == PASSES - 1),
                     )
 
         out2 = out.rearrange("o k a b -> o (k a b)")

@@ -21,6 +21,7 @@ TOKENS = 16384
 PASS = 512
 PASSES = TOKENS // PASS
 O_TILES = O // P
+ON_TENSOR = (0, 2, 3, 5, 6)
 
 FLOPS = 2 * O * K * TOKENS
 BYTES = 2 * 2 * K * TOKENS + 4 * O * K
@@ -31,16 +32,66 @@ def tile_haarwaveletlayer_kernel(tc, x, w_fusion, grad_out, out):
     with ExitStack() as ctx:
         const = ctx.enter_context(tc.tile_pool(name="const", bufs=1))
         loads = ctx.enter_context(tc.tile_pool(name="loads", bufs=3))
-        work = ctx.enter_context(tc.tile_pool(name="work", bufs=3))
+        work = ctx.enter_context(tc.tile_pool(name="work", bufs=2))
         quant = ctx.enter_context(tc.tile_pool(name="quant", bufs=3))
         acc_pool = ctx.enter_context(tc.psum_pool(name="acc", bufs=1))
-        x_banks = ctx.enter_context(tc.psum_pool(name="xbanks", bufs=1))
-        g_banks = ctx.enter_context(tc.psum_pool(name="gbanks", bufs=2))
+        v_banks = ctx.enter_context(tc.psum_pool(name="vbanks", bufs=2))
+        s_banks = ctx.enter_context(tc.psum_pool(name="sbanks", bufs=2))
 
         ident = const.tile([P, P], F32)
         make_identity(nc, ident[:])
 
         acc = [acc_pool.tile([P, K], F32, name="acc%d" % ot) for ot in range(O_TILES)]
+
+        def haar_on_vector(xw, q, gx):
+            top = v_banks.tile([P, 4, P], F32, tag="v")
+            bot = s_banks.tile([P, 4, P], F32, tag="s")
+            for r, bank in ((1, bot), (0, top)):
+                for t in range(4):
+                    s = 512 * q + 256 * (t // 2) + (t % 2)
+                    nc.tensor.transpose(bank[:, t, :], xw[:, r, s : s + 255 : 2], ident[:])
+            bot_sb = work.tile([P, P, 4], F32)
+            nc.scalar.copy(out=bot_sb[:], in_=bot[:].rearrange("p t c -> p c t"))
+            top_px = top[:].bitcast(BF16).rearrange("p t (c h) -> p h c t", h=2)
+            bot_px = bot_sb[:].bitcast(BF16).rearrange("p c (t h) -> p h c t", h=2)
+            sd = work.tile([P, 2, 2, P, 4], F32)
+            nc.vector.tensor_tensor(out=sd[:, 0], in0=top_px, in1=bot_px, op=ADD)
+            nc.vector.tensor_tensor(out=sd[:, 1], in0=top_px, in1=bot_px, op=SUB)
+            nc.vector.tensor_tensor(out=gx[:, 0:2], in0=sd[:, :, 0], in1=sd[:, :, 1], op=ADD)
+            nc.vector.tensor_tensor(out=gx[:, 2:4], in0=sd[:, :, 0], in1=sd[:, :, 1], op=SUB)
+
+        def haar_on_tensor(xs, q, gx):
+            x32 = work.tile([P, 3, 2, 2, 256], F32)
+            for w, (r, sign) in enumerate(((0, 1.0), (1, 1.0), (1, -1.0))):
+                nc.scalar.activation(
+                    out=x32[:, w],
+                    in_=xs[:, r, 1024 * q : 1024 * q + 1024].rearrange("c (m e h) -> c h e m", e=2, h=2),
+                    func=COPY,
+                    scale=sign,
+                )
+            right = work.tile([P, 2, P, 4], F32)
+            for h in (1, 0):
+                for v in range(2):
+                    if h == 1:
+                        bank = s_banks.tile([P, 4, P], F32, tag="s")
+                    else:
+                        bank = v_banks.tile([P, 4, P], F32, tag="v")
+                    for t in range(4):
+                        cols = slice(128 * (t // 2), 128 * (t // 2) + 128)
+                        nc.tensor.matmul(
+                            out=bank[:, t, :], lhsT=x32[:, 0, h, t % 2, cols], rhs=ident[:],
+                            is_transpose=True, start=True, stop=False,
+                        )
+                        nc.tensor.matmul(
+                            out=bank[:, t, :], lhsT=x32[:, 1 + v, h, t % 2, cols], rhs=ident[:],
+                            is_transpose=True, start=False, stop=True,
+                        )
+                    by_channel = bank[:].rearrange("p t c -> p c t")
+                    if h == 1:
+                        nc.scalar.copy(out=right[:, v], in_=by_channel)
+                    else:
+                        nc.vector.tensor_tensor(out=gx[:, v], in0=by_channel, in1=right[:, v], op=ADD)
+                        nc.vector.tensor_tensor(out=gx[:, 2 + v], in0=by_channel, in1=right[:, v], op=SUB)
 
         chunks = [(0, 0, 1), (0, 1, 1), (0, 2, 2), (0, 4, 4)]
         chunks += [(n, f, 4) for n in range(1, IMAGES) for f in (0, 4)]
@@ -69,7 +120,7 @@ def tile_haarwaveletlayer_kernel(tc, x, w_fusion, grad_out, out):
                 gg = work.tile([P, 4 * O], BF16, align_bytes=64)
                 ggw = gg[:].bitcast(F32)
                 for hb in range(2):
-                    gt = g_banks.tile([P, 2, 2, P], F32)
+                    gt = s_banks.tile([P, 2, 2, P], F32, tag="s")
                     for u in range(2):
                         for a in range(2):
                             s = 256 * q + 128 * u
@@ -82,23 +133,11 @@ def tile_haarwaveletlayer_kernel(tc, x, w_fusion, grad_out, out):
                 gsc = quant.tile([P, O], U8, align_bytes=64)
                 nc.vector.quantize_mx(out=gc[:].bitcast(E5M2X4), scales=gsc[:], in_=gg[:])
 
-                top = x_banks.tile([P, 4, P], F32)
-                bot = x_banks.tile([P, 4, P], F32)
-                for r, bank in ((1, bot), (0, top)):
-                    for t in range(4):
-                        s = 512 * q + 256 * (t // 2) + (t % 2)
-                        nc.tensor.transpose(bank[:, t, :], xw[:, r, s : s + 255 : 2], ident[:])
-                bot_sb = work.tile([P, P, 4], F32)
-                nc.scalar.copy(out=bot_sb[:], in_=bot[:].rearrange("p t c -> p c t"))
-
-                top_px = top[:].bitcast(BF16).rearrange("p t (c h) -> p h c t", h=2)
-                bot_px = bot_sb[:].bitcast(BF16).rearrange("p c (t h) -> p h c t", h=2)
-                sd = work.tile([P, 2, 2, P, 4], F32)
-                nc.vector.tensor_tensor(out=sd[:, 0], in0=top_px, in1=bot_px, op=ADD)
-                nc.vector.tensor_tensor(out=sd[:, 1], in0=top_px, in1=bot_px, op=SUB)
                 gx = work.tile([P, 4, P, 4], BF16, align_bytes=64)
-                nc.vector.tensor_tensor(out=gx[:, 0:2], in0=sd[:, :, 0], in1=sd[:, :, 1], op=ADD)
-                nc.gpsimd.tensor_tensor(out=gx[:, 2:4], in0=sd[:, :, 0], in1=sd[:, :, 1], op=SUB)
+                if g % 8 in ON_TENSOR:
+                    haar_on_tensor(xs, q, gx)
+                else:
+                    haar_on_vector(xw, q, gx)
                 xc = quant.tile([P, K], U32, align_bytes=64)
                 xsc = quant.tile([P, K], U8, align_bytes=64)
                 nc.vector.quantize_mx(

@@ -21,7 +21,6 @@ TOKENS = 16384
 PASS = 512
 PASSES = TOKENS // PASS
 O_TILES = O // P
-ON_TENSOR = (0, 2, 3, 5, 6)
 
 FLOPS = 2 * O * K * TOKENS
 BYTES = 2 * 2 * K * TOKENS + 4 * O * K
@@ -32,78 +31,34 @@ def tile_haarwaveletlayer_kernel(tc, x, w_fusion, grad_out, out):
     with ExitStack() as ctx:
         const = ctx.enter_context(tc.tile_pool(name="const", bufs=1))
         loads = ctx.enter_context(tc.tile_pool(name="loads", bufs=3))
-        work = ctx.enter_context(tc.tile_pool(name="work", bufs=2))
-        quant = ctx.enter_context(tc.tile_pool(name="quant", bufs=3))
+        stage = ctx.enter_context(tc.tile_pool(name="stage", bufs=3))
+        grouped = ctx.enter_context(tc.tile_pool(name="grouped", bufs=3))
+        quant = ctx.enter_context(tc.tile_pool(name="quant", bufs=4))
         acc_pool = ctx.enter_context(tc.psum_pool(name="acc", bufs=1))
-        v_banks = ctx.enter_context(tc.psum_pool(name="vbanks", bufs=2))
-        s_banks = ctx.enter_context(tc.psum_pool(name="sbanks", bufs=2))
+        banks = ctx.enter_context(tc.psum_pool(name="banks", bufs=4))
 
         ident = const.tile([P, P], F32)
         make_identity(nc, ident[:])
-
         acc = [acc_pool.tile([P, K], F32, name="acc%d" % ot) for ot in range(O_TILES)]
 
-        def haar_on_vector(xw, q, gx):
-            top = v_banks.tile([P, 4, P], F32, tag="v")
-            bot = s_banks.tile([P, 4, P], F32, tag="s")
-            for r, bank in ((1, bot), (0, top)):
-                for t in range(4):
-                    s = 512 * q + 256 * (t // 2) + (t % 2)
-                    nc.tensor.transpose(bank[:, t, :], xw[:, r, s : s + 255 : 2], ident[:])
-            bot_sb = work.tile([P, P, 4], F32)
-            nc.scalar.copy(out=bot_sb[:], in_=bot[:].rearrange("p t c -> p c t"))
-            top_px = top[:].bitcast(BF16).rearrange("p t (c h) -> p h c t", h=2)
-            bot_px = bot_sb[:].bitcast(BF16).rearrange("p c (t h) -> p h c t", h=2)
-            sd = work.tile([P, 2, 2, P, 4], F32)
-            nc.vector.tensor_tensor(out=sd[:, 0], in0=top_px, in1=bot_px, op=ADD)
-            nc.vector.tensor_tensor(out=sd[:, 1], in0=top_px, in1=bot_px, op=SUB)
-            nc.vector.tensor_tensor(out=gx[:, 0:2], in0=sd[:, :, 0], in1=sd[:, :, 1], op=ADD)
-            nc.vector.tensor_tensor(out=gx[:, 2:4], in0=sd[:, :, 0], in1=sd[:, :, 1], op=SUB)
-
-        def haar_on_tensor(xs, q, gx):
-            x32 = work.tile([P, 3, 2, 2, 256], F32)
-            for w, (r, sign) in enumerate(((0, 1.0), (1, 1.0), (1, -1.0))):
-                nc.scalar.activation(
-                    out=x32[:, w],
-                    in_=xs[:, r, 1024 * q : 1024 * q + 1024].rearrange("c (m e h) -> c h e m", e=2, h=2),
-                    func=COPY,
-                    scale=sign,
-                )
-            right = work.tile([P, 2, P, 4], F32)
-            for h in (1, 0):
-                for v in range(2):
-                    if h == 1:
-                        bank = s_banks.tile([P, 4, P], F32, tag="s")
-                    else:
-                        bank = v_banks.tile([P, 4, P], F32, tag="v")
-                    for t in range(4):
-                        cols = slice(128 * (t // 2), 128 * (t // 2) + 128)
-                        nc.tensor.matmul(
-                            out=bank[:, t, :], lhsT=x32[:, 0, h, t % 2, cols], rhs=ident[:],
-                            is_transpose=True, start=True, stop=False,
-                        )
-                        nc.tensor.matmul(
-                            out=bank[:, t, :], lhsT=x32[:, 1 + v, h, t % 2, cols], rhs=ident[:],
-                            is_transpose=True, start=False, stop=True,
-                        )
-                    by_channel = bank[:].rearrange("p t c -> p c t")
-                    if h == 1:
-                        nc.scalar.copy(out=right[:, v], in_=by_channel)
-                    else:
-                        nc.vector.tensor_tensor(out=gx[:, v], in0=by_channel, in1=right[:, v], op=ADD)
-                        nc.vector.tensor_tensor(out=gx[:, 2 + v], in0=by_channel, in1=right[:, v], op=SUB)
+        ctx.enter_context(tc.manual_schedule())
 
         chunks = [(0, 0, 1), (0, 1, 1), (0, 2, 2), (0, 4, 4)]
         chunks += [(n, f, 4) for n in range(1, IMAGES) for f in (0, 4)]
-        for n, first, count in chunks:
+        src = {}
+        sums = {}
+        ready = {}
+        codes = {}
+
+        def load(n, first, count):
             rows = x[n].rearrange("c (i r) w -> c r i w", r=2)
-            xs = loads.tile([P, 2, 4096], BF16)
+            xs = loads.tile([P, 2, 4096], BF16, name="xs")
             for r in range(2):
                 nc.sync.dma_start(
                     out=xs[:, r, : 1024 * count].rearrange("c (i w) -> c i w", w=128),
                     in_=rows[:, r, 8 * first : 8 * (first + count), :],
                 )
-            gs = loads.tile([P, O_TILES, 2048], BF16)
+            gs = loads.tile([P, O_TILES, 2048], BF16, name="gs")
             for ot in range(O_TILES):
                 nc.sync.dma_start(
                     out=gs[:, ot, : PASS * count],
@@ -111,57 +66,117 @@ def tile_haarwaveletlayer_kernel(tc, x, w_fusion, grad_out, out):
                         :, PASS * first : PASS * (first + count)
                     ],
                 )
-            xw = xs[:].bitcast(F32)
-            gw = gs[:].bitcast(F32)
-
             for q in range(count):
-                g = 8 * n + first + q
+                src[8 * n + first + q] = (xs, gs, q)
 
-                gg = work.tile([P, 4 * O], BF16, align_bytes=64)
-                ggw = gg[:].bitcast(F32)
-                for hb in range(2):
-                    gt = s_banks.tile([P, 2, 2, P], F32, tag="s")
-                    for u in range(2):
-                        for a in range(2):
-                            s = 256 * q + 128 * u
-                            nc.tensor.transpose(gt[:, u, a, :], gw[:, 2 * hb + a, s : s + 128], ident[:])
-                    nc.scalar.copy(
-                        out=ggw[:, 512 * hb : 512 * hb + 512].rearrange("p (o u) -> p o u", u=2),
-                        in_=gt[:].rearrange("p u a o -> p (a o) u"),
+        def first_stage(g):
+            xs, gs, q = src[g]
+            upper = xs[:, 0, 1024 * q : 1024 * q + 1024].rearrange("c (m e h) -> c h e m", e=2, h=2)
+            lower = xs[:, 1, 1024 * q : 1024 * q + 1024].rearrange("c (m e h) -> c h e m", e=2, h=2)
+            sd = stage.tile([P, 2, 2, 2, 256], F32, name="sd")
+            nc.vector.tensor_tensor(out=sd[:, 1], in0=upper, in1=lower, op=SUB)
+            nc.vector.tensor_tensor(out=sd[:, 0], in0=upper, in1=lower, op=ADD)
+            hl = stage.tile([P, 2, 256], F32, name="hl")
+            nc.vector.tensor_tensor(out=hl[:], in0=sd[:, 0, 0], in1=sd[:, 0, 1], op=SUB)
+            sums[g] = [sd, hl, None]
+
+        def negate(g):
+            neg = stage.tile([P, 2, 256], F32, name="neg")
+            nc.scalar.activation(out=neg[:], in_=sums[g][0][:, 1, 1], func=COPY, scale=-1.0)
+            sums[g][2] = neg
+
+        def turn_g(g, hb):
+            xs, gs, q = src[g]
+            gw = gs[:].bitcast(F32)
+            if hb == 0:
+                gg = grouped.tile([P, 4 * O], BF16, name="gg", align_bytes=64)
+                gx = grouped.tile([P, 4, P, 4], BF16, name="gx", align_bytes=64)
+                ready[g] = (gg, gx)
+            gg = ready[g][0]
+            gt = banks.tile([P, 2, 2, P], F32, name="gt", tag="bank")
+            for u in range(2):
+                for a in range(2):
+                    s = 256 * q + 128 * u
+                    nc.tensor.transpose(gt[:, u, a, :], gw[:, 2 * hb + a, s : s + 128], ident[:])
+            nc.scalar.copy(
+                out=gg[:].bitcast(F32)[:, 512 * hb : 512 * hb + 512].rearrange("p (o u) -> p o u", u=2),
+                in_=gt[:].rearrange("p u a o -> p (a o) u"),
+            )
+
+        def turn_band(g, b):
+            sd, hl, neg = sums[g]
+            terms = ((sd[:, 0, 0], sd[:, 0, 1]), (sd[:, 1, 0], sd[:, 1, 1]), (hl[:],), (sd[:, 1, 0], neg[:]))[b]
+            bank = banks.tile([P, 4, P], F32, name="band", tag="bank")
+            for t in range(4):
+                cols = slice(128 * (t // 2), 128 * (t // 2) + 128)
+                for i, term in enumerate(terms):
+                    nc.tensor.matmul(
+                        out=bank[:, t, :], lhsT=term[:, t % 2, cols], rhs=ident[:],
+                        is_transpose=True, start=(i == 0), stop=(i == len(terms) - 1),
                     )
-                gc = quant.tile([P, O], U32, align_bytes=64)
-                gsc = quant.tile([P, O], U8, align_bytes=64)
-                nc.vector.quantize_mx(out=gc[:].bitcast(E5M2X4), scales=gsc[:], in_=gg[:])
+            nc.scalar.activation(
+                out=ready[g][1][:, b], in_=bank[:].rearrange("p t c -> p c t"), func=COPY, scale=0.5
+            )
 
-                gx = work.tile([P, 4, P, 4], BF16, align_bytes=64)
-                if g % 8 in ON_TENSOR:
-                    haar_on_tensor(xs, q, gx)
-                else:
-                    haar_on_vector(xw, q, gx)
-                xc = quant.tile([P, K], U32, align_bytes=64)
-                xsc = quant.tile([P, K], U8, align_bytes=64)
-                nc.vector.quantize_mx(
-                    out=xc[:].bitcast(E4M3X4), scales=xsc[:], in_=gx[:].rearrange("p b c t -> p (b c t)")
+        def quantise(g):
+            gg, gx = ready[g]
+            gc = quant.tile([P, O], U32, name="gc", align_bytes=64)
+            gsc = quant.tile([P, O], U8, name="gsc", align_bytes=64)
+            nc.vector.quantize_mx(out=gc[:].bitcast(E5M2X4), scales=gsc[:], in_=gg[:])
+            xc = quant.tile([P, K], U32, name="xc", align_bytes=64)
+            xsc = quant.tile([P, K], U8, name="xsc", align_bytes=64)
+            nc.vector.quantize_mx(
+                out=xc[:].bitcast(E4M3X4), scales=xsc[:], in_=gx[:].rearrange("p b c t -> p (b c t)")
+            )
+            codes[g] = (gc, gsc, xc, xsc)
+
+        def multiply(g, o_tiles):
+            gc, gsc, xc, xsc = codes[g]
+            for ot in o_tiles:
+                cols = slice(ot * P, (ot + 1) * P)
+                nc.tensor.matmul_mx(
+                    out=acc[ot][:],
+                    lhsT=gc[:, cols].bitcast(E5M2X4),
+                    lhsT_scale=gsc[:, cols],
+                    rhs=xc[:].bitcast(E4M3X4),
+                    rhs_scale=xsc[:],
+                    start=(g == 0),
+                    stop=(g == PASSES - 1),
                 )
 
-                for ot in range(O_TILES):
-                    cols = slice(ot * P, (ot + 1) * P)
-                    nc.tensor.matmul_mx(
-                        out=acc[ot][:],
-                        lhsT=gc[:, cols].bitcast(E5M2X4),
-                        lhsT_scale=gsc[:, cols],
-                        rhs=xc[:].bitcast(E4M3X4),
-                        rhs_scale=xsc[:],
-                        start=(g == 0),
-                        stop=(g == PASSES - 1),
-                    )
+        for c in chunks[:2]:
+            load(*c)
+        waiting = chunks[2:]
+        for s in range(PASSES + 3):
+            while waiting and 8 * waiting[0][0] + waiting[0][1] <= s + 6:
+                load(*waiting[0])
+                waiting = waiting[1:]
+            f = s - 1
+            if 0 <= s - 2 < PASSES:
+                quantise(s - 2)
+            if s < PASSES:
+                first_stage(s)
+            if 0 <= f < PASSES:
+                turn_g(f, 0)
+                turn_g(f, 1)
+                turn_band(f, 3)
+            if s < PASSES:
+                negate(s)
+            if 0 <= s - 3 < PASSES:
+                multiply(s - 3, (2, 3))
+            if 0 <= f < PASSES:
+                turn_band(f, 2)
+                turn_band(f, 0)
+                turn_band(f, 1)
+            if 0 <= s - 2 < PASSES:
+                multiply(s - 2, (0, 1))
 
         out2 = out.rearrange("o k a b -> o (k a b)")
         for ot in range(O_TILES):
-            res = work.tile([P, P, 4], F32)
+            res = grouped.tile([P, P, 4], F32, name="res")
             banded = acc[ot][:].rearrange("p (b c) -> p c b", b=4)
             if ot % 2 == 0:
-                nc.scalar.activation(out=res[:], in_=banded, func=COPY, scale=0.5)
+                nc.scalar.copy(out=res[:], in_=banded)
             else:
-                nc.vector.tensor_scalar_mul(res[:], banded, 0.5)
+                nc.vector.tensor_copy(out=res[:], in_=banded)
             nc.sync.dma_start(out=out2[ot * P : (ot + 1) * P, :], in_=res[:].rearrange("p c b -> p (c b)"))

@@ -47,17 +47,16 @@ def tile_haarwaveletlayer_kernel(tc, x, w_fusion, grad_out, out):
         chunks += [(n, f, 4) for n in range(1, IMAGES) for f in (0, 4)]
         src = {}
         sums = {}
+        diffs = {}
         ready = {}
         codes = {}
 
         def load(n, first, count):
-            rows = x[n].rearrange("c (i r) w -> c r i w", r=2)
-            xs = loads.tile([P, 2, 4096], BF16, name="xs")
-            for r in range(2):
-                nc.sync.dma_start(
-                    out=xs[:, r, : 1024 * count].rearrange("c (i w) -> c i w", w=128),
-                    in_=rows[:, r, 8 * first : 8 * (first + count), :],
-                )
+            xs = loads.tile([P, 4 * 2048], BF16, name="xs")
+            nc.sync.dma_start(
+                out=xs[:, : 2048 * count],
+                in_=x[n][:, 16 * first : 16 * (first + count), :].rearrange("c h w -> c (h w)"),
+            )
             gs = loads.tile([P, O_TILES, 2048], BF16, name="gs")
             for ot in range(O_TILES):
                 nc.sync.dma_start(
@@ -71,19 +70,19 @@ def tile_haarwaveletlayer_kernel(tc, x, w_fusion, grad_out, out):
 
         def first_stage(g):
             xs, gs, q = src[g]
-            upper = xs[:, 0, 1024 * q : 1024 * q + 1024].rearrange("c (m e h) -> c h e m", e=2, h=2)
-            lower = xs[:, 1, 1024 * q : 1024 * q + 1024].rearrange("c (m e h) -> c h e m", e=2, h=2)
-            sd = stage.tile([P, 2, 2, 2, 256], F32, name="sd")
-            nc.vector.tensor_tensor(out=sd[:, 1], in0=upper, in1=lower, op=SUB)
-            nc.vector.tensor_tensor(out=sd[:, 0], in0=upper, in1=lower, op=ADD)
-            hl = stage.tile([P, 2, 256], F32, name="hl")
-            nc.vector.tensor_tensor(out=hl[:], in0=sd[:, 0, 0], in1=sd[:, 0, 1], op=SUB)
-            sums[g] = [sd, hl, None]
+            px = xs[:, 2048 * q : 2048 * q + 2048].rearrange("c (i r j k) -> c r k i j", i=8, r=2, j=32, k=4)
+            sd = stage.tile([P, 2, 4, 256], F32, name="sd")
+            for s_, op in ((0, ADD), (1, SUB)):
+                nc.vector.tensor_tensor(
+                    out=sd[:, s_].rearrange("c k (i j) -> c k i j", i=8), in0=px[:, 0], in1=px[:, 1], op=op
+                )
+            sums[g] = sd
 
-        def negate(g):
-            neg = stage.tile([P, 2, 256], F32, name="neg")
-            nc.scalar.activation(out=neg[:], in_=sums[g][0][:, 1, 1], func=COPY, scale=-1.0)
-            sums[g][2] = neg
+        def second_stage(g):
+            ab = stage.tile([P, 2, 256, 2], BF16, name="ab")
+            v = sums[g][:].rearrange("c s (e h) m -> c h s m e", h=2)
+            nc.vector.tensor_tensor(out=ab[:], in0=v[:, 0], in1=v[:, 1], op=SUB)
+            diffs[g] = ab
 
         def turn_g(g, hb):
             xs, gs, q = src[g]
@@ -103,19 +102,29 @@ def tile_haarwaveletlayer_kernel(tc, x, w_fusion, grad_out, out):
                 in_=gt[:].rearrange("p u a o -> p (a o) u"),
             )
 
-        def turn_band(g, b):
-            sd, hl, neg = sums[g]
-            terms = ((sd[:, 0, 0], sd[:, 0, 1]), (sd[:, 1, 0], sd[:, 1, 1]), (hl[:],), (sd[:, 1, 0], neg[:]))[b]
+        def turn_sum(g, b):
+            sd = sums[g]
             bank = banks.tile([P, 4, P], F32, name="band", tag="bank")
             for t in range(4):
-                cols = slice(128 * (t // 2), 128 * (t // 2) + 128)
-                for i, term in enumerate(terms):
+                u, e = divmod(t, 2)
+                for h in range(2):
                     nc.tensor.matmul(
-                        out=bank[:, t, :], lhsT=term[:, t % 2, cols], rhs=ident[:],
-                        is_transpose=True, start=(i == 0), stop=(i == len(terms) - 1),
+                        out=bank[:, t, :], lhsT=sd[:, b, 2 * e + h, 128 * u : 128 * u + 128], rhs=ident[:],
+                        is_transpose=True, start=(h == 0), stop=(h == 1),
                     )
-            nc.scalar.activation(
-                out=ready[g][1][:, b], in_=bank[:].rearrange("p t c -> p c t"), func=COPY, scale=0.5
+            nc.scalar.copy(out=ready[g][1][:, b], in_=bank[:].rearrange("p t c -> p c t"))
+
+        def turn_diffs(g):
+            words = diffs[g][:].rearrange("c s m e -> c (s m e)").bitcast(F32)
+            bank = banks.tile([P, 2, 2, P], F32, name="dw", tag="bank")
+            for s_ in range(2):
+                for u in range(2):
+                    w0 = 256 * s_ + 128 * u
+                    nc.tensor.transpose(bank[:, s_, u, :], words[:, w0 : w0 + 128], ident[:])
+            gxw = ready[g][1][:].rearrange("p b c t -> p (b c t)").bitcast(F32)
+            nc.scalar.copy(
+                out=gxw[:, 512:1024].rearrange("p (s c u) -> p s c u", s=2, u=2),
+                in_=bank[:].rearrange("p s u c -> p s c u"),
             )
 
         def quantise(g):
@@ -147,36 +156,32 @@ def tile_haarwaveletlayer_kernel(tc, x, w_fusion, grad_out, out):
         for c in chunks[:2]:
             load(*c)
         waiting = chunks[2:]
-        for s in range(PASSES + 3):
+        for s in range(PASSES + 2):
             while waiting and 8 * waiting[0][0] + waiting[0][1] <= s + 6:
                 load(*waiting[0])
                 waiting = waiting[1:]
             f = s - 1
             if 0 <= s - 2 < PASSES:
                 quantise(s - 2)
+            if 0 <= f < PASSES:
+                second_stage(f)
             if s < PASSES:
                 first_stage(s)
             if 0 <= f < PASSES:
                 turn_g(f, 0)
                 turn_g(f, 1)
-                turn_band(f, 3)
-            if s < PASSES:
-                negate(s)
-            if 0 <= s - 3 < PASSES:
-                multiply(s - 3, (2, 3))
-            if 0 <= f < PASSES:
-                turn_band(f, 2)
-                turn_band(f, 0)
-                turn_band(f, 1)
+                turn_sum(f, 0)
+                turn_sum(f, 1)
+                turn_diffs(f)
             if 0 <= s - 2 < PASSES:
-                multiply(s - 2, (0, 1))
+                multiply(s - 2, (0, 1, 2, 3))
 
         out2 = out.rearrange("o k a b -> o (k a b)")
         for ot in range(O_TILES):
             res = grouped.tile([P, P, 4], F32, name="res")
             banded = acc[ot][:].rearrange("p (b c) -> p c b", b=4)
             if ot % 2 == 0:
-                nc.scalar.copy(out=res[:], in_=banded)
+                nc.scalar.activation(out=res[:], in_=banded, func=COPY, scale=0.5)
             else:
-                nc.vector.tensor_copy(out=res[:], in_=banded)
+                nc.vector.tensor_scalar_mul(out=res[:], in0=banded, scalar1=0.5)
             nc.sync.dma_start(out=out2[ot * P : (ot + 1) * P, :], in_=res[:].rearrange("p c b -> p (c b)"))

@@ -48,6 +48,7 @@ def tile_haarwaveletlayer_kernel(tc, x, w_fusion, grad_out, out):
         src = {}
         sums = {}
         diffs = {}
+        negs = {}
         ready = {}
         codes = {}
 
@@ -79,10 +80,16 @@ def tile_haarwaveletlayer_kernel(tc, x, w_fusion, grad_out, out):
             sums[g] = sd
 
         def second_stage(g):
-            ab = stage.tile([P, 2, 256, 2], BF16, name="ab")
-            v = sums[g][:].rearrange("c s (e h) m -> c h s m e", h=2)
+            ab = stage.tile([P, 256, 2], BF16, name="ab")
+            v = sums[g][:, 0].rearrange("c (e h) m -> c h m e", h=2)
             nc.vector.tensor_tensor(out=ab[:], in0=v[:, 0], in1=v[:, 1], op=SUB)
             diffs[g] = ab
+
+        def negate(g):
+            neg = stage.tile([P, 2, 256], F32, name="neg")
+            v = sums[g][:, 1].rearrange("c (e h) m -> c h e m", h=2)
+            nc.scalar.activation(out=neg[:], in_=v[:, 1], func=COPY, scale=-1.0)
+            negs[g] = neg
 
         def turn_g(g, hb):
             xs, gs, q = src[g]
@@ -115,17 +122,28 @@ def tile_haarwaveletlayer_kernel(tc, x, w_fusion, grad_out, out):
             nc.scalar.copy(out=ready[g][1][:, b], in_=bank[:].rearrange("p t c -> p c t"))
 
         def turn_diffs(g):
-            words = diffs[g][:].rearrange("c s m e -> c (s m e)").bitcast(F32)
-            bank = banks.tile([P, 2, 2, P], F32, name="dw", tag="bank")
-            for s_ in range(2):
-                for u in range(2):
-                    w0 = 256 * s_ + 128 * u
-                    nc.tensor.transpose(bank[:, s_, u, :], words[:, w0 : w0 + 128], ident[:])
+            words = diffs[g][:].rearrange("c m e -> c (m e)").bitcast(F32)
+            bank = banks.tile([P, 2, P], F32, name="dw", tag="bank")
+            for u in range(2):
+                nc.tensor.transpose(bank[:, u, :], words[:, 128 * u : 128 * u + 128], ident[:])
             gxw = ready[g][1][:].rearrange("p b c t -> p (b c t)").bitcast(F32)
             nc.scalar.copy(
-                out=gxw[:, 512:1024].rearrange("p (s c u) -> p s c u", s=2, u=2),
-                in_=bank[:].rearrange("p s u c -> p s c u"),
+                out=gxw[:, 512:768].rearrange("p (c u) -> p c u", u=2),
+                in_=bank[:].rearrange("p u c -> p c u"),
             )
+
+        def turn_hh(g):
+            sd = sums[g]
+            neg = negs[g]
+            bank = banks.tile([P, 4, P], F32, name="hh", tag="bank")
+            for t in range(4):
+                u, e = divmod(t, 2)
+                cols = slice(128 * u, 128 * u + 128)
+                for i, term in enumerate((sd[:, 1, 2 * e, cols], neg[:, e, cols])):
+                    nc.tensor.matmul(
+                        out=bank[:, t, :], lhsT=term, rhs=ident[:], is_transpose=True, start=(i == 0), stop=(i == 1)
+                    )
+            nc.scalar.copy(out=ready[g][1][:, 3], in_=bank[:].rearrange("p t c -> p c t"))
 
         def quantise(g):
             gg, gx = ready[g]
@@ -168,11 +186,13 @@ def tile_haarwaveletlayer_kernel(tc, x, w_fusion, grad_out, out):
             if s < PASSES:
                 first_stage(s)
             if 0 <= f < PASSES:
+                negate(f)
                 turn_g(f, 0)
                 turn_g(f, 1)
                 turn_sum(f, 0)
                 turn_sum(f, 1)
                 turn_diffs(f)
+                turn_hh(f)
             if 0 <= s - 2 < PASSES:
                 multiply(s - 2, (0, 1, 2, 3))
 

@@ -109,17 +109,20 @@ def tile_haarwaveletlayer_kernel(tc, x, w_fusion, grad_out, out):
                 in_=gt[:].rearrange("p u a o -> p (a o) u"),
             )
 
-        def turn_sum(g, b):
+        def turn_sums(g):
             sd = sums[g]
-            bank = banks.tile([P, 4, P], F32, name="band", tag="bank")
+            bank_ll = banks.tile([P, 4, P], F32, name="bank_ll", tag="bank")
+            bank_lh = banks.tile([P, 4, P], F32, name="bank_lh", tag="bank")
             for t in range(4):
                 u, e = divmod(t, 2)
                 for h in range(2):
-                    nc.tensor.matmul(
-                        out=bank[:, t, :], lhsT=sd[:, b, 2 * e + h, 128 * u : 128 * u + 128], rhs=ident[:],
-                        is_transpose=True, start=(h == 0), stop=(h == 1),
-                    )
-            nc.scalar.copy(out=ready[g][1][:, b], in_=bank[:].rearrange("p t c -> p c t"))
+                    for b, bank in enumerate((bank_ll, bank_lh)):
+                        nc.tensor.matmul(
+                            out=bank[:, t, :], lhsT=sd[:, b, 2 * e + h, 128 * u : 128 * u + 128], rhs=ident[:],
+                            is_transpose=True, start=(h == 0), stop=(h == 1),
+                        )
+            for b, bank in enumerate((bank_ll, bank_lh)):
+                nc.scalar.copy(out=ready[g][1][:, b], in_=bank[:].rearrange("p t c -> p c t"))
 
         def turn_diffs(g):
             words = diffs[g][:].rearrange("c m e -> c (m e)").bitcast(F32)
@@ -189,8 +192,7 @@ def tile_haarwaveletlayer_kernel(tc, x, w_fusion, grad_out, out):
                 negate(f)
                 turn_g(f, 0)
                 turn_g(f, 1)
-                turn_sum(f, 0)
-                turn_sum(f, 1)
+                turn_sums(f)
                 turn_diffs(f)
                 turn_hh(f)
             if 0 <= s - 2 < PASSES:

@@ -25,15 +25,20 @@ O_TILES = O // P
 FLOPS = 2 * O * K * TOKENS
 BYTES = 2 * 2 * K * TOKENS + 4 * O * K
 
+SIZES = [1, 1] + [2] * 14 + [1, 1]
+G_AHEAD = 1
+LOADS_AHEAD = 3
+HH_ON_VECTOR_EVERY = 0
+
 
 def tile_haarwaveletlayer_kernel(tc, x, w_fusion, grad_out, out):
     nc = tc.nc
     with ExitStack() as ctx:
         const = ctx.enter_context(tc.tile_pool(name="const", bufs=1))
-        loads = ctx.enter_context(tc.tile_pool(name="loads", bufs=3))
+        loads = ctx.enter_context(tc.tile_pool(name="loads", bufs=4))
         stage = ctx.enter_context(tc.tile_pool(name="stage", bufs=3))
-        grouped = ctx.enter_context(tc.tile_pool(name="grouped", bufs=3))
-        quant = ctx.enter_context(tc.tile_pool(name="quant", bufs=4))
+        grouped = ctx.enter_context(tc.tile_pool(name="grouped", bufs=4))
+        quant = ctx.enter_context(tc.tile_pool(name="quant", bufs=3))
         acc_pool = ctx.enter_context(tc.psum_pool(name="acc", bufs=1))
         banks = ctx.enter_context(tc.psum_pool(name="banks", bufs=4))
 
@@ -43,22 +48,32 @@ def tile_haarwaveletlayer_kernel(tc, x, w_fusion, grad_out, out):
 
         ctx.enter_context(tc.manual_schedule())
 
-        chunks = [(0, 0, 1), (0, 1, 1), (0, 2, 2), (0, 4, 4)]
-        chunks += [(n, f, 4) for n in range(1, IMAGES) for f in (0, 4)]
-        src = {}
+        first_of = [sum(SIZES[:i]) for i in range(len(SIZES))]
+        group_of = {}
+        for i, n in enumerate(SIZES):
+            for q in range(n):
+                group_of[first_of[i] + q] = (i, q)
+        xs_of = {}
+        gs_of = {}
         sums = {}
         diffs = {}
         negs = {}
-        ready = {}
+        gg_of = {}
+        gx_of = {}
         codes = {}
 
-        def load(n, first, count):
-            xs = loads.tile([P, 4 * 2048], BF16, name="xs")
+        def hh_on_vector(i):
+            return HH_ON_VECTOR_EVERY > 0 and SIZES[i] == 2 and i % HH_ON_VECTOR_EVERY == HH_ON_VECTOR_EVERY - 1
+
+        def load(i):
+            n, first = divmod(first_of[i], 8)
+            count = SIZES[i]
+            xs = loads.tile([P, 2 * 2048], BF16, name="xs")
             nc.sync.dma_start(
                 out=xs[:, : 2048 * count],
                 in_=x[n][:, 16 * first : 16 * (first + count), :].rearrange("c h w -> c (h w)"),
             )
-            gs = loads.tile([P, O_TILES, 2048], BF16, name="gs")
+            gs = loads.tile([P, O_TILES, 2 * PASS], BF16, name="gs")
             for ot in range(O_TILES):
                 nc.sync.dma_start(
                     out=gs[:, ot, : PASS * count],
@@ -66,137 +81,164 @@ def tile_haarwaveletlayer_kernel(tc, x, w_fusion, grad_out, out):
                         :, PASS * first : PASS * (first + count)
                     ],
                 )
-            for q in range(count):
-                src[8 * n + first + q] = (xs, gs, q)
+            xs_of[i] = xs
+            gs_of[i] = gs
 
-        def first_stage(g):
-            xs, gs, q = src[g]
-            px = xs[:, 2048 * q : 2048 * q + 2048].rearrange("c (i r j k) -> c r k i j", i=8, r=2, j=32, k=4)
-            sd = stage.tile([P, 2, 4, 256], F32, name="sd")
+        def first_stage(i):
+            n = SIZES[i]
+            px = xs_of[i][:, : 2048 * n].rearrange("c (i r j k) -> c r k i j", i=8 * n, r=2, j=32, k=4)
+            sd = stage.tile([P, 2, 4, 512], F32, name="sd")
             for s_, op in ((0, ADD), (1, SUB)):
                 nc.vector.tensor_tensor(
-                    out=sd[:, s_].rearrange("c k (i j) -> c k i j", i=8), in0=px[:, 0], in1=px[:, 1], op=op
+                    out=sd[:, s_, :, : 256 * n].rearrange("c k (i j) -> c k i j", i=8 * n),
+                    in0=px[:, 0], in1=px[:, 1], op=op,
                 )
-            sums[g] = sd
+            sums[i] = sd
 
-        def second_stage(g):
-            ab = stage.tile([P, 256, 2], BF16, name="ab")
-            v = sums[g][:, 0].rearrange("c (e h) m -> c h m e", h=2)
-            nc.vector.tensor_tensor(out=ab[:], in0=v[:, 0], in1=v[:, 1], op=SUB)
-            diffs[g] = ab
+        def second_stage(i):
+            n = SIZES[i]
+            bands = 2 if hh_on_vector(i) else 1
+            ab = stage.tile([P, 2, 512, 2], BF16, name="ab")
+            v = sums[i][:, :bands, :, : 256 * n].rearrange("c s (e h) m -> c h s m e", h=2)
+            nc.vector.tensor_tensor(out=ab[:, :bands, : 256 * n, :], in0=v[:, 0], in1=v[:, 1], op=SUB)
+            diffs[i] = ab
 
-        def negate(g):
+        def negate(f):
+            i, q = group_of[f]
             neg = stage.tile([P, 2, 256], F32, name="neg")
-            v = sums[g][:, 1].rearrange("c (e h) m -> c h e m", h=2)
+            v = sums[i][:, 1, :, 256 * q : 256 * q + 256].rearrange("c (e h) m -> c h e m", h=2)
             nc.scalar.activation(out=neg[:], in_=v[:, 1], func=COPY, scale=-1.0)
-            negs[g] = neg
+            negs[f] = neg
 
-        def turn_g(g, hb):
-            xs, gs, q = src[g]
-            gw = gs[:].bitcast(F32)
-            if hb == 0:
-                gg = grouped.tile([P, 4 * O], BF16, name="gg", align_bytes=64)
-                gx = grouped.tile([P, 4, P, 4], BF16, name="gx", align_bytes=64)
-                ready[g] = (gg, gx)
-            gg = ready[g][0]
-            gt = banks.tile([P, 2, 2, P], F32, name="gt", tag="bank")
-            for u in range(2):
-                for a in range(2):
-                    s = 256 * q + 128 * u
-                    nc.tensor.transpose(gt[:, u, a, :], gw[:, 2 * hb + a, s : s + 128], ident[:])
-            nc.scalar.copy(
-                out=gg[:].bitcast(F32)[:, 512 * hb : 512 * hb + 512].rearrange("p (o u) -> p o u", u=2),
-                in_=gt[:].rearrange("p u a o -> p (a o) u"),
-            )
+        def turn_g(f):
+            i, q = group_of[f]
+            if q == 0:
+                gg_new = grouped.tile([P, 2, 4 * O], BF16, name="gg", align_bytes=64)
+                gg_of[i] = gg_new
+            gw = gs_of[i][:].bitcast(F32)
+            ggw = gg_of[i][:, q, :].bitcast(F32)
+            for hb in range(2):
+                gt = banks.tile([P, 2, 2, P], F32, name="gt", tag="bank")
+                for u in range(2):
+                    for a in range(2):
+                        w0 = 256 * q + 128 * u
+                        nc.tensor.transpose(gt[:, u, a, :], gw[:, 2 * hb + a, w0 : w0 + 128], ident[:])
+                nc.scalar.copy(
+                    out=ggw[:, 512 * hb : 512 * hb + 512].rearrange("p (o u) -> p o u", u=2),
+                    in_=gt[:].rearrange("p u a o -> p (a o) u"),
+                )
 
-        def turn_sums(g):
-            sd = sums[g]
+        def turn_sums(f):
+            i, q = group_of[f]
+            if q == 0:
+                gx_new = grouped.tile([P, 2, 4, P, 4], BF16, name="gx", align_bytes=64)
+                gx_of[i] = gx_new
+            sd = sums[i]
             bank_ll = banks.tile([P, 4, P], F32, name="bank_ll", tag="bank")
             bank_lh = banks.tile([P, 4, P], F32, name="bank_lh", tag="bank")
             for t in range(4):
                 u, e = divmod(t, 2)
+                m0 = 256 * q + 128 * u
                 for h in range(2):
                     for b, bank in enumerate((bank_ll, bank_lh)):
                         nc.tensor.matmul(
-                            out=bank[:, t, :], lhsT=sd[:, b, 2 * e + h, 128 * u : 128 * u + 128], rhs=ident[:],
+                            out=bank[:, t, :], lhsT=sd[:, b, 2 * e + h, m0 : m0 + 128], rhs=ident[:],
                             is_transpose=True, start=(h == 0), stop=(h == 1),
                         )
             for b, bank in enumerate((bank_ll, bank_lh)):
-                nc.scalar.copy(out=ready[g][1][:, b], in_=bank[:].rearrange("p t c -> p c t"))
+                nc.scalar.copy(out=gx_of[i][:, q, b], in_=bank[:].rearrange("p t c -> p c t"))
 
-        def turn_diffs(g):
-            words = diffs[g][:].rearrange("c m e -> c (m e)").bitcast(F32)
-            bank = banks.tile([P, 2, P], F32, name="dw", tag="bank")
-            for u in range(2):
-                nc.tensor.transpose(bank[:, u, :], words[:, 128 * u : 128 * u + 128], ident[:])
-            gxw = ready[g][1][:].rearrange("p b c t -> p (b c t)").bitcast(F32)
-            nc.scalar.copy(
-                out=gxw[:, 512:768].rearrange("p (c u) -> p c u", u=2),
-                in_=bank[:].rearrange("p u c -> p c u"),
-            )
-
-        def turn_hh(g):
-            sd = sums[g]
-            neg = negs[g]
+        def turn_hh(f):
+            i, q = group_of[f]
+            sd = sums[i]
+            neg = negs[f]
             bank = banks.tile([P, 4, P], F32, name="hh", tag="bank")
             for t in range(4):
                 u, e = divmod(t, 2)
-                cols = slice(128 * u, 128 * u + 128)
-                for i, term in enumerate((sd[:, 1, 2 * e, cols], neg[:, e, cols])):
+                terms = (sd[:, 1, 2 * e, 256 * q + 128 * u : 256 * q + 128 * u + 128], neg[:, e, 128 * u : 128 * u + 128])
+                for j, term in enumerate(terms):
                     nc.tensor.matmul(
-                        out=bank[:, t, :], lhsT=term, rhs=ident[:], is_transpose=True, start=(i == 0), stop=(i == 1)
+                        out=bank[:, t, :], lhsT=term, rhs=ident[:], is_transpose=True, start=(j == 0), stop=(j == 1)
                     )
-            nc.scalar.copy(out=ready[g][1][:, 3], in_=bank[:].rearrange("p t c -> p c t"))
+            nc.scalar.copy(out=gx_of[i][:, q, 3], in_=bank[:].rearrange("p t c -> p c t"))
 
-        def quantise(g):
-            gg, gx = ready[g]
-            gc = quant.tile([P, O], U32, name="gc", align_bytes=64)
-            gsc = quant.tile([P, O], U8, name="gsc", align_bytes=64)
-            nc.vector.quantize_mx(out=gc[:].bitcast(E5M2X4), scales=gsc[:], in_=gg[:])
-            xc = quant.tile([P, K], U32, name="xc", align_bytes=64)
-            xsc = quant.tile([P, K], U8, name="xsc", align_bytes=64)
-            nc.vector.quantize_mx(
-                out=xc[:].bitcast(E4M3X4), scales=xsc[:], in_=gx[:].rearrange("p b c t -> p (b c t)")
+        def turn_diffs(f):
+            i, q = group_of[f]
+            bands = 2 if hh_on_vector(i) else 1
+            words = diffs[i][:].rearrange("c s m e -> c (s m e)").bitcast(F32)
+            bank = banks.tile([P, 2, 2, P], F32, name="dw", tag="bank")
+            for s_ in range(bands):
+                for u in range(2):
+                    w0 = 512 * s_ + 256 * q + 128 * u
+                    nc.tensor.transpose(bank[:, s_, u, :], words[:, w0 : w0 + 128], ident[:])
+            gxw = gx_of[i][:, q].rearrange("p b c t -> p (b c t)").bitcast(F32)
+            nc.scalar.copy(
+                out=gxw[:, 512 : 512 + 256 * bands].rearrange("p (s c u) -> p s c u", s=bands, u=2),
+                in_=bank[:, :bands].rearrange("p s u c -> p s c u"),
             )
-            codes[g] = (gc, gsc, xc, xsc)
 
-        def multiply(g, o_tiles):
-            gc, gsc, xc, xsc = codes[g]
-            for ot in o_tiles:
-                cols = slice(ot * P, (ot + 1) * P)
+        def quantise(i):
+            n = SIZES[i]
+            gc = quant.tile([P, 2 * O], U32, name="gc", align_bytes=64)
+            gsc = quant.tile([P, 2 * O], U8, name="gsc", align_bytes=64)
+            nc.vector.quantize_mx(
+                out=gc[:, : O * n].bitcast(E5M2X4), scales=gsc[:, : O * n],
+                in_=gg_of[i][:, :n].rearrange("p q w -> p (q w)"),
+            )
+            xc = quant.tile([P, 2 * K], U32, name="xc", align_bytes=64)
+            xsc = quant.tile([P, 2 * K], U8, name="xsc", align_bytes=64)
+            nc.vector.quantize_mx(
+                out=xc[:, : K * n].bitcast(E4M3X4), scales=xsc[:, : K * n],
+                in_=gx_of[i][:, :n].rearrange("p q b c t -> p (q b c t)"),
+            )
+            codes[i] = (gc, gsc, xc, xsc)
+
+        def multiply(f):
+            i, q = group_of[f]
+            gc, gsc, xc, xsc = codes[i]
+            for ot in range(O_TILES):
+                cols = slice(q * O + ot * P, q * O + (ot + 1) * P)
                 nc.tensor.matmul_mx(
                     out=acc[ot][:],
                     lhsT=gc[:, cols].bitcast(E5M2X4),
                     lhsT_scale=gsc[:, cols],
-                    rhs=xc[:].bitcast(E4M3X4),
-                    rhs_scale=xsc[:],
-                    start=(g == 0),
-                    stop=(g == PASSES - 1),
+                    rhs=xc[:, q * K : (q + 1) * K].bitcast(E4M3X4),
+                    rhs_scale=xsc[:, q * K : (q + 1) * K],
+                    start=(f == 0),
+                    stop=(f == PASSES - 1),
                 )
 
-        for c in chunks[:2]:
-            load(*c)
-        waiting = chunks[2:]
-        for s in range(PASSES + 2):
-            while waiting and 8 * waiting[0][0] + waiting[0][1] <= s + 6:
-                load(*waiting[0])
-                waiting = waiting[1:]
-            f = s - 1
-            if 0 <= s - 2 < PASSES:
-                quantise(s - 2)
-            if 0 <= f < PASSES:
-                second_stage(f)
-            if s < PASSES:
-                first_stage(s)
-            if 0 <= f < PASSES:
-                negate(f)
-                turn_g(f, 0)
-                turn_g(f, 1)
+        groups = len(SIZES)
+        for i in range(LOADS_AHEAD):
+            load(i)
+        for f in range(G_AHEAD):
+            turn_g(f)
+        pending = []
+        for i in range(groups):
+            if i + LOADS_AHEAD < groups:
+                load(i + LOADS_AHEAD)
+            first_stage(i)
+            second_stage(i)
+            if i > 0:
+                quantise(i - 1)
+                pending.extend(range(first_of[i - 1], first_of[i - 1] + SIZES[i - 1]))
+            for q in range(SIZES[i]):
+                f = first_of[i] + q
+                if not hh_on_vector(i):
+                    negate(f)
+                if f + G_AHEAD < PASSES:
+                    turn_g(f + G_AHEAD)
                 turn_sums(f)
+                if not hh_on_vector(i):
+                    turn_hh(f)
                 turn_diffs(f)
-                turn_hh(f)
-            if 0 <= s - 2 < PASSES:
-                multiply(s - 2, (0, 1, 2, 3))
+                if pending and pending[0] <= f - (2 * SIZES[group_of[pending[0]][0]] - 1):
+                    multiply(pending[0])
+                    pending = pending[1:]
+        quantise(groups - 1)
+        pending.extend(range(first_of[groups - 1], PASSES))
+        for f in pending:
+            multiply(f)
 
         out2 = out.rearrange("o k a b -> o (k a b)")
         for ot in range(O_TILES):

@@ -25,9 +25,11 @@ O_TILES = O // P
 FLOPS = 2 * O * K * TOKENS
 BYTES = 2 * 2 * K * TOKENS + 4 * O * K
 
-SIZES = [1, 1] + [2] * 14 + [1, 1]
+SIZES = [1] * 32
+GMAX = max(SIZES)
+Q_BEHIND = 2
 G_AHEAD = 1
-LOADS_AHEAD = 3
+LOADS_AHEAD = 5
 HH_ON_VECTOR_EVERY = 0
 
 
@@ -35,10 +37,10 @@ def tile_haarwaveletlayer_kernel(tc, x, w_fusion, grad_out, out):
     nc = tc.nc
     with ExitStack() as ctx:
         const = ctx.enter_context(tc.tile_pool(name="const", bufs=1))
-        loads = ctx.enter_context(tc.tile_pool(name="loads", bufs=4))
+        loads = ctx.enter_context(tc.tile_pool(name="loads", bufs=7))
         stage = ctx.enter_context(tc.tile_pool(name="stage", bufs=3))
-        grouped = ctx.enter_context(tc.tile_pool(name="grouped", bufs=4))
-        quant = ctx.enter_context(tc.tile_pool(name="quant", bufs=3))
+        grouped = ctx.enter_context(tc.tile_pool(name="grouped", bufs=5))
+        quant = ctx.enter_context(tc.tile_pool(name="quant", bufs=4))
         acc_pool = ctx.enter_context(tc.psum_pool(name="acc", bufs=1))
         banks = ctx.enter_context(tc.psum_pool(name="banks", bufs=4))
 
@@ -63,17 +65,20 @@ def tile_haarwaveletlayer_kernel(tc, x, w_fusion, grad_out, out):
         codes = {}
 
         def hh_on_vector(i):
-            return HH_ON_VECTOR_EVERY > 0 and SIZES[i] == 2 and i % HH_ON_VECTOR_EVERY == HH_ON_VECTOR_EVERY - 1
+            return i == len(SIZES) - 1
 
         def load(i):
             n, first = divmod(first_of[i], 8)
             count = SIZES[i]
-            xs = loads.tile([P, 2 * 2048], BF16, name="xs")
-            nc.sync.dma_start(
-                out=xs[:, : 2048 * count],
-                in_=x[n][:, 16 * first : 16 * (first + count), :].rearrange("c h w -> c (h w)"),
-            )
-            gs = loads.tile([P, O_TILES, 2 * PASS], BF16, name="gs")
+            xs = loads.tile([P, GMAX * 2048], BF16, name="xs")
+            pieces = 2 if i == 0 else 1
+            rows = 16 * count // pieces
+            for piece in range(pieces):
+                nc.sync.dma_start(
+                    out=xs[:, 128 * rows * piece : 128 * rows * (piece + 1)],
+                    in_=x[n][:, 16 * first + rows * piece : 16 * first + rows * (piece + 1), :].rearrange("c h w -> c (h w)"),
+                )
+            gs = loads.tile([P, O_TILES, GMAX * PASS], BF16, name="gs")
             for ot in range(O_TILES):
                 nc.sync.dma_start(
                     out=gs[:, ot, : PASS * count],
@@ -87,18 +92,21 @@ def tile_haarwaveletlayer_kernel(tc, x, w_fusion, grad_out, out):
         def first_stage(i):
             n = SIZES[i]
             px = xs_of[i][:, : 2048 * n].rearrange("c (i r j k) -> c r k i j", i=8 * n, r=2, j=32, k=4)
-            sd = stage.tile([P, 2, 4, 512], F32, name="sd")
-            for s_, op in ((0, ADD), (1, SUB)):
-                nc.vector.tensor_tensor(
-                    out=sd[:, s_, :, : 256 * n].rearrange("c k (i j) -> c k i j", i=8 * n),
-                    in0=px[:, 0], in1=px[:, 1], op=op,
-                )
+            sd = stage.tile([P, 2, 4, GMAX * 256], F32, name="sd")
+            pieces = 2 if i == 0 else 1
+            ti = 8 * n // pieces
+            for piece in range(pieces):
+                for s_, op in ((0, ADD), (1, SUB)):
+                    nc.vector.tensor_tensor(
+                        out=sd[:, s_, :, 32 * ti * piece : 32 * ti * (piece + 1)].rearrange("c k (i j) -> c k i j", i=ti),
+                        in0=px[:, 0, :, ti * piece : ti * (piece + 1), :], in1=px[:, 1, :, ti * piece : ti * (piece + 1), :], op=op,
+                    )
             sums[i] = sd
 
         def second_stage(i):
             n = SIZES[i]
             bands = 2 if hh_on_vector(i) else 1
-            ab = stage.tile([P, 2, 512, 2], BF16, name="ab")
+            ab = stage.tile([P, 2, GMAX * 256, 2], BF16, name="ab")
             v = sums[i][:, :bands, :, : 256 * n].rearrange("c s (e h) m -> c h s m e", h=2)
             nc.vector.tensor_tensor(out=ab[:, :bands, : 256 * n, :], in0=v[:, 0], in1=v[:, 1], op=SUB)
             diffs[i] = ab
@@ -113,7 +121,7 @@ def tile_haarwaveletlayer_kernel(tc, x, w_fusion, grad_out, out):
         def turn_g(f):
             i, q = group_of[f]
             if q == 0:
-                gg_new = grouped.tile([P, 2, 4 * O], BF16, name="gg", align_bytes=64)
+                gg_new = grouped.tile([P, GMAX, 4 * O], BF16, name="gg", align_bytes=64)
                 gg_of[i] = gg_new
             gw = gs_of[i][:].bitcast(F32)
             ggw = gg_of[i][:, q, :].bitcast(F32)
@@ -131,7 +139,7 @@ def tile_haarwaveletlayer_kernel(tc, x, w_fusion, grad_out, out):
         def turn_sums(f):
             i, q = group_of[f]
             if q == 0:
-                gx_new = grouped.tile([P, 2, 4, P, 4], BF16, name="gx", align_bytes=64)
+                gx_new = grouped.tile([P, GMAX, 4, P, 4], BF16, name="gx", align_bytes=64)
                 gx_of[i] = gx_new
             sd = sums[i]
             bank_ll = banks.tile([P, 4, P], F32, name="bank_ll", tag="bank")
@@ -146,7 +154,10 @@ def tile_haarwaveletlayer_kernel(tc, x, w_fusion, grad_out, out):
                             is_transpose=True, start=(h == 0), stop=(h == 1),
                         )
             for b, bank in enumerate((bank_ll, bank_lh)):
-                nc.scalar.copy(out=gx_of[i][:, q, b], in_=bank[:].rearrange("p t c -> p c t"))
+                if b == 1 and f == PASSES - 1:
+                    nc.vector.tensor_copy(out=gx_of[i][:, q, b], in_=bank[:].rearrange("p t c -> p c t"))
+                else:
+                    nc.scalar.copy(out=gx_of[i][:, q, b], in_=bank[:].rearrange("p t c -> p c t"))
 
         def turn_hh(f):
             i, q = group_of[f]
@@ -169,7 +180,7 @@ def tile_haarwaveletlayer_kernel(tc, x, w_fusion, grad_out, out):
             bank = banks.tile([P, 2, 2, P], F32, name="dw", tag="bank")
             for s_ in range(bands):
                 for u in range(2):
-                    w0 = 512 * s_ + 256 * q + 128 * u
+                    w0 = GMAX * 256 * s_ + 256 * q + 128 * u
                     nc.tensor.transpose(bank[:, s_, u, :], words[:, w0 : w0 + 128], ident[:])
             gxw = gx_of[i][:, q].rearrange("p b c t -> p (b c t)").bitcast(F32)
             nc.scalar.copy(
@@ -179,14 +190,14 @@ def tile_haarwaveletlayer_kernel(tc, x, w_fusion, grad_out, out):
 
         def quantise(i):
             n = SIZES[i]
-            gc = quant.tile([P, 2 * O], U32, name="gc", align_bytes=64)
-            gsc = quant.tile([P, 2 * O], U8, name="gsc", align_bytes=64)
+            gc = quant.tile([P, GMAX * O], U32, name="gc", align_bytes=64)
+            gsc = quant.tile([P, GMAX * O], U8, name="gsc", align_bytes=64)
             nc.vector.quantize_mx(
                 out=gc[:, : O * n].bitcast(E5M2X4), scales=gsc[:, : O * n],
                 in_=gg_of[i][:, :n].rearrange("p q w -> p (q w)"),
             )
-            xc = quant.tile([P, 2 * K], U32, name="xc", align_bytes=64)
-            xsc = quant.tile([P, 2 * K], U8, name="xsc", align_bytes=64)
+            xc = quant.tile([P, GMAX * K], U32, name="xc", align_bytes=64)
+            xsc = quant.tile([P, GMAX * K], U8, name="xsc", align_bytes=64)
             nc.vector.quantize_mx(
                 out=xc[:, : K * n].bitcast(E4M3X4), scales=xsc[:, : K * n],
                 in_=gx_of[i][:, :n].rearrange("p q b c t -> p (q b c t)"),
@@ -219,9 +230,9 @@ def tile_haarwaveletlayer_kernel(tc, x, w_fusion, grad_out, out):
                 load(i + LOADS_AHEAD)
             first_stage(i)
             second_stage(i)
-            if i > 0:
-                quantise(i - 1)
-                pending.extend(range(first_of[i - 1], first_of[i - 1] + SIZES[i - 1]))
+            if i >= Q_BEHIND:
+                quantise(i - Q_BEHIND)
+                pending.extend(range(first_of[i - Q_BEHIND], first_of[i - Q_BEHIND] + SIZES[i - Q_BEHIND]))
             for q in range(SIZES[i]):
                 f = first_of[i] + q
                 if not hh_on_vector(i):
@@ -232,13 +243,15 @@ def tile_haarwaveletlayer_kernel(tc, x, w_fusion, grad_out, out):
                 if not hh_on_vector(i):
                     turn_hh(f)
                 turn_diffs(f)
-                if pending and pending[0] <= f - (2 * SIZES[group_of[pending[0]][0]] - 1):
+                if pending:
                     multiply(pending[0])
                     pending = pending[1:]
-        quantise(groups - 1)
-        pending.extend(range(first_of[groups - 1], PASSES))
-        for f in pending:
-            multiply(f)
+        for i in range(groups - Q_BEHIND, groups):
+            quantise(i)
+            pending.extend(range(first_of[i], first_of[i] + SIZES[i]))
+            for f in pending:
+                multiply(f)
+            pending = []
 
         out2 = out.rearrange("o k a b -> o (k a b)")
         for ot in range(O_TILES):

@@ -44,8 +44,9 @@ def tile_haarwaveletlayer_kernel(tc, x, w_fusion, grad_out, out):
         acc_pool = ctx.enter_context(tc.psum_pool(name="acc", bufs=1))
         banks = ctx.enter_context(tc.psum_pool(name="banks", bufs=4))
 
-        ident = const.tile([P, P], F32)
-        make_identity(nc, ident[:])
+        ident_tile = const.tile([P, P + 32], F32, align_bytes=256)
+        ident = ident_tile[:, 32 : 32 + P]
+        make_identity(nc, ident)
         acc = [acc_pool.tile([P, K], F32, name="acc%d" % ot) for ot in range(O_TILES)]
 
         ctx.enter_context(tc.manual_schedule())
@@ -130,7 +131,7 @@ def tile_haarwaveletlayer_kernel(tc, x, w_fusion, grad_out, out):
                 for u in range(2):
                     for a in range(2):
                         w0 = 256 * q + 128 * u
-                        nc.tensor.transpose(gt[:, u, a, :], gw[:, 2 * hb + a, w0 : w0 + 128], ident[:])
+                        nc.tensor.transpose(gt[:, u, a, :], gw[:, 2 * hb + a, w0 : w0 + 128], ident)
                 nc.scalar.copy(
                     out=ggw[:, 512 * hb : 512 * hb + 512].rearrange("p (o u) -> p o u", u=2),
                     in_=gt[:].rearrange("p u a o -> p (a o) u"),
@@ -150,7 +151,7 @@ def tile_haarwaveletlayer_kernel(tc, x, w_fusion, grad_out, out):
                 for h in range(2):
                     for b, bank in enumerate((bank_ll, bank_lh)):
                         nc.tensor.matmul(
-                            out=bank[:, t, :], lhsT=sd[:, b, 2 * e + h, m0 : m0 + 128], rhs=ident[:],
+                            out=bank[:, t, :], lhsT=sd[:, b, 2 * e + h, m0 : m0 + 128], rhs=ident,
                             is_transpose=True, start=(h == 0), stop=(h == 1),
                         )
             for b, bank in enumerate((bank_ll, bank_lh)):
@@ -169,7 +170,7 @@ def tile_haarwaveletlayer_kernel(tc, x, w_fusion, grad_out, out):
                 terms = (sd[:, 1, 2 * e, 256 * q + 128 * u : 256 * q + 128 * u + 128], neg[:, e, 128 * u : 128 * u + 128])
                 for j, term in enumerate(terms):
                     nc.tensor.matmul(
-                        out=bank[:, t, :], lhsT=term, rhs=ident[:], is_transpose=True, start=(j == 0), stop=(j == 1)
+                        out=bank[:, t, :], lhsT=term, rhs=ident, is_transpose=True, start=(j == 0), stop=(j == 1)
                     )
             nc.scalar.copy(out=gx_of[i][:, q, 3], in_=bank[:].rearrange("p t c -> p c t"))
 
@@ -181,7 +182,7 @@ def tile_haarwaveletlayer_kernel(tc, x, w_fusion, grad_out, out):
             for s_ in range(bands):
                 for u in range(2):
                     w0 = GMAX * 256 * s_ + 256 * q + 128 * u
-                    nc.tensor.transpose(bank[:, s_, u, :], words[:, w0 : w0 + 128], ident[:])
+                    nc.tensor.transpose(bank[:, s_, u, :], words[:, w0 : w0 + 128], ident)
             gxw = gx_of[i][:, q].rearrange("p b c t -> p (b c t)").bitcast(F32)
             nc.scalar.copy(
                 out=gxw[:, 512 : 512 + 256 * bands].rearrange("p (s c u) -> p s c u", s=bands, u=2),
@@ -190,14 +191,18 @@ def tile_haarwaveletlayer_kernel(tc, x, w_fusion, grad_out, out):
 
         def quantise(i):
             n = SIZES[i]
-            gc = quant.tile([P, GMAX * O], U32, name="gc", align_bytes=64)
-            gsc = quant.tile([P, GMAX * O], U8, name="gsc", align_bytes=64)
+            gc_tile = quant.tile([P, GMAX * O + 64], U32, name="gc", align_bytes=256)
+            gsc_tile = quant.tile([P, GMAX * O + 256], U8, name="gsc", align_bytes=256)
+            gc = gc_tile[:, 32 : 32 + GMAX * O]
+            gsc = gsc_tile[:, 192 : 192 + GMAX * O]
             nc.vector.quantize_mx(
                 out=gc[:, : O * n].bitcast(E5M2X4), scales=gsc[:, : O * n],
                 in_=gg_of[i][:, :n].rearrange("p q w -> p (q w)"),
             )
-            xc = quant.tile([P, GMAX * K], U32, name="xc", align_bytes=64)
-            xsc = quant.tile([P, GMAX * K], U8, name="xsc", align_bytes=64)
+            xc_tile = quant.tile([P, GMAX * K], U32, name="xc", align_bytes=256)
+            xsc_tile = quant.tile([P, GMAX * K + 256], U8, name="xsc", align_bytes=256)
+            xc = xc_tile[:, : GMAX * K]
+            xsc = xsc_tile[:, 64 : 64 + GMAX * K]
             nc.vector.quantize_mx(
                 out=xc[:, : K * n].bitcast(E4M3X4), scales=xsc[:, : K * n],
                 in_=gx_of[i][:, :n].rearrange("p q b c t -> p (q b c t)"),

from contextlib import ExitStack

import concourse.mybir as mybir
from concourse.masks import make_identity

F32 = mybir.dt.float32
BF16 = mybir.dt.bfloat16
U32 = mybir.dt.uint32
U8 = mybir.dt.uint8
E4M3X4 = mybir.dt.float8_e4m3fn_x4
E5M2X4 = mybir.dt.float8_e5m2_x4
ADD = mybir.AluOpType.add
SUB = mybir.AluOpType.subtract
COPY = mybir.ActivationFunctionType.Copy

P = 128
IMAGES = 4
O = 512
K = 512
TOKENS = 16384
PASS = 512
PASSES = TOKENS // PASS
O_TILES = O // P

FLOPS = 2 * O * K * TOKENS
BYTES = 2 * 2 * K * TOKENS + 4 * O * K

SIZES = [1] * 32
GMAX = max(SIZES)
Q_BEHIND = 2
G_AHEAD = 1
LOADS_AHEAD = 5
HH_ON_VECTOR_EVERY = 0


def tile_haarwaveletlayer_kernel(tc, x, w_fusion, grad_out, out):
    nc = tc.nc
    with ExitStack() as ctx:
        const = ctx.enter_context(tc.tile_pool(name="const", bufs=1))
        loads = ctx.enter_context(tc.tile_pool(name="loads", bufs=7))
        stage = ctx.enter_context(tc.tile_pool(name="stage", bufs=3))
        grouped = ctx.enter_context(tc.tile_pool(name="grouped", bufs=5))
        quant = ctx.enter_context(tc.tile_pool(name="quant", bufs=4))
        acc_pool = ctx.enter_context(tc.psum_pool(name="acc", bufs=1))
        banks = ctx.enter_context(tc.psum_pool(name="banks", bufs=4))

        ident_tile = const.tile([P, P + 32], F32, align_bytes=256)
        ident = ident_tile[:, 32 : 32 + P]
        make_identity(nc, ident)
        acc = [acc_pool.tile([P, K], F32, name="acc%d" % ot) for ot in range(O_TILES)]

        ctx.enter_context(tc.manual_schedule())

        first_of = [sum(SIZES[:i]) for i in range(len(SIZES))]
        group_of = {}
        for i, n in enumerate(SIZES):
            for q in range(n):
                group_of[first_of[i] + q] = (i, q)
        xs_of = {}
        gs_of = {}
        sums = {}
        diffs = {}
        negs = {}
        gg_of = {}
        gx_of = {}
        codes = {}

        def hh_on_vector(i):
            return i == len(SIZES) - 1

        def load(i):
            n, first = divmod(first_of[i], 8)
            count = SIZES[i]
            xs = loads.tile([P, GMAX * 2048], BF16, name="xs")
            pieces = 2 if i == 0 else 1
            rows = 16 * count // pieces
            for piece in range(pieces):
                nc.sync.dma_start(
                    out=xs[:, 128 * rows * piece : 128 * rows * (piece + 1)],
                    in_=x[n][:, 16 * first + rows * piece : 16 * first + rows * (piece + 1), :].rearrange("c h w -> c (h w)"),
                )
            gs = loads.tile([P, O_TILES, GMAX * PASS], BF16, name="gs")
            for ot in range(O_TILES):
                nc.sync.dma_start(
                    out=gs[:, ot, : PASS * count],
                    in_=grad_out[n, ot * P : (ot + 1) * P].rearrange("o i j -> o (i j)")[
                        :, PASS * first : PASS * (first + count)
                    ],
                )
            xs_of[i] = xs
            gs_of[i] = gs

        def first_stage(i):
            n = SIZES[i]
            px = xs_of[i][:, : 2048 * n].rearrange("c (i r j k) -> c r k i j", i=8 * n, r=2, j=32, k=4)
            sd = stage.tile([P, 2, 4, GMAX * 256], F32, name="sd")
            pieces = 2 if i == 0 else 1
            ti = 8 * n // pieces
            for piece in range(pieces):
                for s_, op in ((0, ADD), (1, SUB)):
                    nc.vector.tensor_tensor(
                        out=sd[:, s_, :, 32 * ti * piece : 32 * ti * (piece + 1)].rearrange("c k (i j) -> c k i j", i=ti),
                        in0=px[:, 0, :, ti * piece : ti * (piece + 1), :], in1=px[:, 1, :, ti * piece : ti * (piece + 1), :], op=op,
                    )
            sums[i] = sd

        def second_stage(i):
            n = SIZES[i]
            bands = 2 if hh_on_vector(i) else 1
            ab = stage.tile([P, 2, GMAX * 256, 2], BF16, name="ab")
            v = sums[i][:, :bands, :, : 256 * n].rearrange("c s (e h) m -> c h s m e", h=2)
            nc.vector.tensor_tensor(out=ab[:, :bands, : 256 * n, :], in0=v[:, 0], in1=v[:, 1], op=SUB)
            diffs[i] = ab

        def negate(f):
            i, q = group_of[f]
            neg = stage.tile([P, 2, 256], F32, name="neg")
            v = sums[i][:, 1, :, 256 * q : 256 * q + 256].rearrange("c (e h) m -> c h e m", h=2)
            nc.scalar.activation(out=neg[:], in_=v[:, 1], func=COPY, scale=-1.0)
            negs[f] = neg

        def turn_g(f):
            i, q = group_of[f]
            if q == 0:
                gg_new = grouped.tile([P, GMAX, 4 * O], BF16, name="gg", align_bytes=64)
                gg_of[i] = gg_new
            gw = gs_of[i][:].bitcast(F32)
            ggw = gg_of[i][:, q, :].bitcast(F32)
            for hb in range(2):
                gt = banks.tile([P, 2, 2, P], F32, name="gt", tag="bank")
                for u in range(2):
                    for a in range(2):
                        w0 = 256 * q + 128 * u
                        nc.tensor.transpose(gt[:, u, a, :], gw[:, 2 * hb + a, w0 : w0 + 128], ident)
                nc.scalar.copy(
                    out=ggw[:, 512 * hb : 512 * hb + 512].rearrange("p (o u) -> p o u", u=2),
                    in_=gt[:].rearrange("p u a o -> p (a o) u"),
                )

        def turn_sums(f):
            i, q = group_of[f]
            if q == 0:
                gx_new = grouped.tile([P, GMAX, 4, P, 4], BF16, name="gx", align_bytes=64)
                gx_of[i] = gx_new
            sd = sums[i]
            bank_ll = banks.tile([P, 4, P], F32, name="bank_ll", tag="bank")
            bank_lh = banks.tile([P, 4, P], F32, name="bank_lh", tag="bank")
            for t in range(4):
                u, e = divmod(t, 2)
                m0 = 256 * q + 128 * u
                for h in range(2):
                    for b, bank in enumerate((bank_ll, bank_lh)):
                        nc.tensor.matmul(
                            out=bank[:, t, :], lhsT=sd[:, b, 2 * e + h, m0 : m0 + 128], rhs=ident,
                            is_transpose=True, start=(h == 0), stop=(h == 1),
                        )
            for b, bank in enumerate((bank_ll, bank_lh)):
                if b == 1 and f == PASSES - 1:
                    nc.vector.tensor_copy(out=gx_of[i][:, q, b], in_=bank[:].rearrange("p t c -> p c t"))
                else:
                    nc.scalar.copy(out=gx_of[i][:, q, b], in_=bank[:].rearrange("p t c -> p c t"))

        def turn_hh(f):
            i, q = group_of[f]
            sd = sums[i]
            neg = negs[f]
            bank = banks.tile([P, 4, P], F32, name="hh", tag="bank")
            for t in range(4):
                u, e = divmod(t, 2)
                terms = (sd[:, 1, 2 * e, 256 * q + 128 * u : 256 * q + 128 * u + 128], neg[:, e, 128 * u : 128 * u + 128])
                for j, term in enumerate(terms):
                    nc.tensor.matmul(
                        out=bank[:, t, :], lhsT=term, rhs=ident, is_transpose=True, start=(j == 0), stop=(j == 1)
                    )
            nc.scalar.copy(out=gx_of[i][:, q, 3], in_=bank[:].rearrange("p t c -> p c t"))

        def turn_diffs(f):
            i, q = group_of[f]
            bands = 2 if hh_on_vector(i) else 1
            words = diffs[i][:].rearrange("c s m e -> c (s m e)").bitcast(F32)
            bank = banks.tile([P, 2, 2, P], F32, name="dw", tag="bank")
            for s_ in range(bands):
                for u in range(2):
                    w0 = GMAX * 256 * s_ + 256 * q + 128 * u
                    nc.tensor.transpose(bank[:, s_, u, :], words[:, w0 : w0 + 128], ident)
            gxw = gx_of[i][:, q].rearrange("p b c t -> p (b c t)").bitcast(F32)
            nc.scalar.copy(
                out=gxw[:, 512 : 512 + 256 * bands].rearrange("p (s c u) -> p s c u", s=bands, u=2),
                in_=bank[:, :bands].rearrange("p s u c -> p s c u"),
            )

        def quantise(i):
            n = SIZES[i]
            gc_tile = quant.tile([P, GMAX * O + 64], U32, name="gc", align_bytes=256)
            gsc_tile = quant.tile([P, GMAX * O + 256], U8, name="gsc", align_bytes=256)
            gc = gc_tile[:, 32 : 32 + GMAX * O]
            gsc = gsc_tile[:, 192 : 192 + GMAX * O]
            nc.vector.quantize_mx(
                out=gc[:, : O * n].bitcast(E5M2X4), scales=gsc[:, : O * n],
                in_=gg_of[i][:, :n].rearrange("p q w -> p (q w)"),
            )
            xc_tile = quant.tile([P, GMAX * K], U32, name="xc", align_bytes=256)
            xsc_tile = quant.tile([P, GMAX * K + 256], U8, name="xsc", align_bytes=256)
            xc = xc_tile[:, : GMAX * K]
            xsc = xsc_tile[:, 64 : 64 + GMAX * K]
            nc.vector.quantize_mx(
                out=xc[:, : K * n].bitcast(E4M3X4), scales=xsc[:, : K * n],
                in_=gx_of[i][:, :n].rearrange("p q b c t -> p (q b c t)"),
            )
            codes[i] = (gc, gsc, xc, xsc)

        def multiply(f):
            i, q = group_of[f]
            gc, gsc, xc, xsc = codes[i]
            for ot in range(O_TILES):
                cols = slice(q * O + ot * P, q * O + (ot + 1) * P)
                nc.tensor.matmul_mx(
                    out=acc[ot][:],
                    lhsT=gc[:, cols].bitcast(E5M2X4),
                    lhsT_scale=gsc[:, cols],
                    rhs=xc[:, q * K : (q + 1) * K].bitcast(E4M3X4),
                    rhs_scale=xsc[:, q * K : (q + 1) * K],
                    start=(f == 0),
                    stop=(f == PASSES - 1),
                )

        groups = len(SIZES)
        for i in range(LOADS_AHEAD):
            load(i)
        for f in range(G_AHEAD):
            turn_g(f)
        pending = []
        for i in range(groups):
            if i + LOADS_AHEAD < groups:
                load(i + LOADS_AHEAD)
            first_stage(i)
            second_stage(i)
            if i >= Q_BEHIND:
                quantise(i - Q_BEHIND)
                pending.extend(range(first_of[i - Q_BEHIND], first_of[i - Q_BEHIND] + SIZES[i - Q_BEHIND]))
            for q in range(SIZES[i]):
                f = first_of[i] + q
                if not hh_on_vector(i):
                    negate(f)
                if f + G_AHEAD < PASSES:
                    turn_g(f + G_AHEAD)
                turn_sums(f)
                if not hh_on_vector(i):
                    turn_hh(f)
                turn_diffs(f)
                if pending:
                    multiply(pending[0])
                    pending = pending[1:]
        for i in range(groups - Q_BEHIND, groups):
            quantise(i)
            pending.extend(range(first_of[i], first_of[i] + SIZES[i]))
            for f in pending:
                multiply(f)
            pending = []

        out2 = out.rearrange("o k a b -> o (k a b)")
        for ot in range(O_TILES):
            res = grouped.tile([P, P, 4], F32, name="res")
            banded = acc[ot][:].rearrange("p (b c) -> p c b", b=4)
            if ot % 2 == 0:
                nc.scalar.activation(out=res[:], in_=banded, func=COPY, scale=0.5)
            else:
                nc.vector.tensor_scalar_mul(out=res[:], in0=banded, scalar1=0.5)
            nc.sync.dma_start(out=out2[ot * P : (ot + 1) * P, :], in_=res[:].rearrange("p c b -> p (c b)"))
